import numpy as np
import ml_dtypes


def mxq(x, axis, fmt="e4m3"):
    dtype, down = {"e4m3": (ml_dtypes.float8_e4m3fn, 7), "e5m2": (ml_dtypes.float8_e5m2, 14)}[fmt]
    v = np.moveaxis(np.asarray(x, np.float32).astype(ml_dtypes.bfloat16).astype(np.float64), axis, -1)
    blocks = v.reshape(v.shape[:-1] + (-1, 32))
    amax = np.abs(blocks).max(-1, keepdims=True)
    byte = np.maximum(np.where(amax > 0, np.frexp(amax)[1] - 1 + 127, 0) - down, 1)
    scale = np.exp2(byte - 127.0)
    codes = (blocks / scale).astype(np.float32).astype(dtype).astype(np.float64)
    return np.moveaxis((codes * scale).reshape(v.shape), -1, axis)


WIDE = False


def mx_kscale(k):
    if not WIDE:
        return np.ones(k)
    levels = np.array([10, -10, 5, -5, 0])
    a = np.random.permutation(np.resize(levels, k // 512 * 4)).reshape(k // 512, 4)
    idx = np.arange(k)
    return np.exp2(a[idx // 512, idx % 128 // 32])


BF16 = ml_dtypes.bfloat16


def bf(x):
    return np.asarray(x, np.float32).astype(BF16)


def f64(x):
    return np.asarray(x).astype(np.float64)


B, DIN, F, NCLS, NV = 4096, 1024, 128, 18, 3
S_NM = 2.0 / np.sqrt(DIN)
S_AN = 0.25 * np.sqrt(F / DIN)


def draw_view():
    s = mx_kscale(DIN)
    x = bf(np.random.standard_normal((B, DIN)) * s)
    w_nm = bf(np.random.standard_normal((DIN, F)) * S_NM / s[:, None])
    w_an = bf(np.random.standard_normal((DIN, F)) * S_AN / s[:, None])
    return x, w_nm, w_an


def setup_inputs():
    x_dash, Wd_nm, Wd_an = draw_view()
    x_rear, Wr_nm, Wr_an = draw_view()
    x_right, Wt_nm, Wt_an = draw_view()
    return {"x_dash": x_dash, "x_rear": x_rear, "x_right": x_right,
            "Wd_nm": Wd_nm, "Wd_an": Wd_an, "Wr_nm": Wr_nm, "Wr_an": Wr_an, "Wt_nm": Wt_nm, "Wt_an": Wt_an}


def branch(x, w_nm, w_an):
    xq = mxq(f64(x), 1, "e4m3")
    nm = xq @ mxq(f64(w_nm), 0, "e4m3")
    an = xq @ mxq(f64(w_an), 0, "e4m3")
    return np.mean(an, axis=1, keepdims=True) * nm


def reference(x_dash, x_rear, x_right, Wd_nm, Wd_an, Wr_nm, Wr_an, Wt_nm, Wt_an):
    v = np.concatenate([branch(x_dash, Wd_nm, Wd_an), branch(x_rear, Wr_nm, Wr_an), branch(x_right, Wt_nm, Wt_an)], axis=1)
    return v.reshape(v.shape[0], F, NV).mean(axis=-1)

@@ -1,0 +1,197 @@
+from contextlib import ExitStack
+
+import concourse.mybir as mybir
+from concourse.masks import make_identity
+
+F32 = mybir.dt.float32
+BF16 = mybir.dt.bfloat16
+U32 = mybir.dt.uint32
+U8 = mybir.dt.uint8
+FP8X4 = mybir.dt.float8_e4m3fn_x4
+ADD = mybir.AluOpType.add
+MULT = mybir.AluOpType.mult
+
+P = 128
+B = 4096
+K = 1024
+F = 128
+VIEWS = 3
+PACK = 4
+K_PASS = P * PACK
+PASSES = K // K_PASS
+WORDS = K // 2
+ROW_TILES = B // P
+CHUNK = 4
+GROUPS = ROW_TILES // CHUNK
+CHUNKS = GROUPS * VIEWS
+PAIR = 2
+X_BUFS = 8
+T_BANKS = 4
+
+FLOPS = 2 * B * K * F * 2 * VIEWS
+
+
+def tile_fusion_r3d_pa_t_kernel(
+    tc, x_dash, x_rear, x_right, Wd_nm, Wd_an, Wr_nm, Wr_an, Wt_nm, Wt_an, out
+):
+    nc = tc.nc
+    xs = (x_dash, x_rear, x_right)
+    weights = ((Wd_nm, Wd_an), (Wr_nm, Wr_an), (Wt_nm, Wt_an))
+
+    x_rows = [x.rearrange("(p t) k -> p (t k)", t=ROW_TILES) for x in xs]
+    out_rows = out.rearrange("(p t) j -> p (t j)", t=ROW_TILES)
+
+    with ExitStack() as ctx:
+        const = ctx.enter_context(tc.tile_pool(name="const", bufs=1))
+        x_pool = ctx.enter_context(tc.tile_pool(name="x", bufs=X_BUFS))
+        work = ctx.enter_context(tc.tile_pool(name="work", bufs=3))
+        psum_t = ctx.enter_context(tc.psum_pool(name="psum_t", bufs=T_BANKS))
+        psum_m = ctx.enter_context(tc.psum_pool(name="psum_m", bufs=8 - T_BANKS))
+
+        identity = const.tile([P, P], F32)
+        make_identity(nc, identity[:])
+
+        x_tiles = {}
+        x_codes = {}
+        x_scales = {}
+        w_raw = {}
+        w_codes = {}
+        w_scales = {}
+        products = {}
+        branches = {}
+
+        def load_x(c):
+            group, view = divmod(c, VIEWS)
+            x_sb = x_pool.tile([P, CHUNK * K], BF16, name="x_sb")
+            nc.sync.dma_start(
+                out=x_sb[:], in_=x_rows[view][:, group * CHUNK * K : (group + 1) * CHUNK * K]
+            )
+            x_tiles[c] = x_sb
+
+        def load_weights(view):
+            raw = const.tile([P, 2, 2 * PACK, F], BF16, name="w_raw%d" % view)
+            for w in range(2):
+                nc.sync.dma_start(
+                    out=raw[:, w].rearrange("p (a e) f -> p a (e f)", e=2),
+                    in_=weights[view][w].rearrange("(a p e) f -> p a (e f)", p=P, e=2),
+                )
+            w_raw[view] = raw
+
+        def quantise_weights(view):
+            grouped = const.tile([P, PASSES, 2, F, PACK], BF16, name="w_grouped%d" % view, align_bytes=64)
+            for g in range(PASSES):
+                nc.vector.tensor_copy(
+                    out=grouped[:, g],
+                    in_=w_raw[view][:, :, g * PACK : (g + 1) * PACK, :].rearrange("p w t f -> p w f t"),
+                )
+            codes = const.tile([P, PASSES * 2 * F], U32, name="w_codes%d" % view, align_bytes=64)
+            scales = const.tile([P, PASSES * 2 * F], U8, name="w_scales%d" % view, align_bytes=64)
+            nc.vector.quantize_mx(
+                out=codes[:].bitcast(FP8X4),
+                scales=scales[:],
+                in_=grouped[:].rearrange("p g w f t -> p (g w f t)"),
+            )
+            w_codes[view] = codes
+            w_scales[view] = scales
+
+        def transpose_x(c):
+            x_words = x_tiles.pop(c)[:].bitcast(F32)
+            grouped = work.tile([P, CHUNK * K], BF16, name="x_grouped", align_bytes=64)
+            grouped_words = grouped[:].bitcast(F32)
+            for i in range(CHUNK):
+                xt = psum_t.tile([P, WORDS], F32, name="xt")
+                for a in range(WORDS // P):
+                    nc.tensor.transpose(
+                        xt[:, a * P : (a + 1) * P],
+                        x_words[:, i * WORDS + a * P : i * WORDS + (a + 1) * P],
+                        identity[:],
+                    )
+                nc.scalar.copy(
+                    out=grouped_words[:, i * WORDS : (i + 1) * WORDS].rearrange(
+                        "p (g r u) -> p g r u", g=PASSES, u=2
+                    ),
+                    in_=xt[:].rearrange("p (g u r) -> p g r u", g=PASSES, u=2),
+                )
+            return grouped
+
+        def quantise_x(c, grouped):
+            codes = work.tile([P, CHUNK * PASSES * P], U32, name="x_codes", align_bytes=64)
+            scales = work.tile([P, CHUNK * PASSES * P], U8, name="x_scales", align_bytes=64)
+            nc.vector.quantize_mx(out=codes[:].bitcast(FP8X4), scales=scales[:], in_=grouped[:])
+            x_codes[c] = codes
+            x_scales[c] = scales
+
+        def multiply(c):
+            view = c % VIEWS
+            codes = x_codes.pop(c)
+            scales = x_scales.pop(c)
+            products[c] = []
+            for h in range(CHUNK // PAIR):
+                acc = psum_m.tile([P, PAIR, 2 * F], F32, name="acc")
+                for i in range(PAIR):
+                    for g in range(PASSES):
+                        rows = slice(((h * PAIR + i) * PASSES + g) * P, ((h * PAIR + i) * PASSES + g + 1) * P)
+                        cols = slice(g * 2 * F, (g + 1) * 2 * F)
+                        nc.tensor.matmul_mx(
+                            out=acc[:, i, :],
+                            lhsT=codes[:, rows].bitcast(FP8X4),
+                            lhsT_scale=scales[:, rows],
+                            rhs=w_codes[view][:, cols].bitcast(FP8X4),
+                            rhs_scale=w_scales[view][:, cols],
+                            start=(g == 0),
+                            stop=(g == PASSES - 1),
+                        )
+                products[c].append(acc)
+
+        def scale_branch(c):
+            group, view = divmod(c, VIEWS)
+            if view == 0:
+                branches[group] = work.tile([P, CHUNK, VIEWS * F], F32, name="v_sb")
+            v_sb = branches[group]
+            accs = products.pop(c)
+            sums = []
+            for acc in accs:
+                an_sum = work.tile([P, PAIR], F32, name="an_sum", bufs=6)
+                nc.vector.tensor_reduce(out=an_sum[:], in_=acc[:, :, F : 2 * F], axis=mybir.AxisListType.X, op=ADD)
+                sums.append(an_sum)
+            for h, acc in enumerate(accs):
+                nc.vector.scalar_tensor_tensor(
+                    out=v_sb[:, h * PAIR : (h + 1) * PAIR, view * F : (view + 1) * F],
+                    in0=acc[:, :, 0:F],
+                    scalar=1.0 / (F * VIEWS),
+                    in1=sums[h][:].unsqueeze(2).to_broadcast([P, PAIR, F]),
+                    op0=MULT,
+                    op1=MULT,
+                )
+
+        def average_and_store(group):
+            v_sb = branches.pop(group)
+            out_sb = work.tile([P, CHUNK * F], F32, name="out_sb")
+            nc.vector.tensor_reduce(
+                out=out_sb[:],
+                in_=v_sb[:].rearrange("p i (j s) -> p (i j) s", s=VIEWS),
+                axis=mybir.AxisListType.X,
+                op=ADD,
+            )
+            nc.gpsimd.dma_start(out=out_rows[:, group * CHUNK * F : (group + 1) * CHUNK * F], in_=out_sb[:])
+
+        with tc.manual_schedule():
+            for c in range(X_BUFS):
+                load_x(c)
+                if c < VIEWS:
+                    load_weights(c)
+            grouped = {}
+            for s in range(CHUNKS + 2):
+                if s < CHUNKS:
+                    grouped[s] = transpose_x(s)
+                    if s + X_BUFS < CHUNKS:
+                        load_x(s + X_BUFS)
+                if s < VIEWS:
+                    quantise_weights(s)
+                if 1 <= s <= CHUNKS:
+                    quantise_x(s - 1, grouped.pop(s - 1))
+                    multiply(s - 1)
+                if s >= 2:
+                    scale_branch(s - 2)
+                    if (s - 2) % VIEWS == VIEWS - 1:
+                        average_and_store((s - 2) // VIEWS)

@@ -166,14 +166,13 @@ def tile_fusion_r3d_pa_t_kernel(
 
         def average_and_store(group):
             v_sb = branches.pop(group)
-            out_sb = work.tile([P, CHUNK * F], F32, name="out_sb")
-            nc.vector.tensor_reduce(
-                out=out_sb[:],
-                in_=v_sb[:].rearrange("p i (j s) -> p (i j) s", s=VIEWS),
-                axis=mybir.AxisListType.X,
-                op=ADD,
-            )
-            nc.gpsimd.dma_start(out=out_rows[:, group * CHUNK * F : (group + 1) * CHUNK * F], in_=out_sb[:])
+            out_sb = work.tile([P, CHUNK, F], F32, name="out_sb")
+            thirds = v_sb[:].rearrange("p i (j s) -> p i j s", s=VIEWS)
+            for h in range(CHUNK // PAIR):
+                pair = slice(h * PAIR, (h + 1) * PAIR)
+                nc.gpsimd.tensor_tensor(out=out_sb[:, pair], in0=thirds[:, pair, :, 0], in1=thirds[:, pair, :, 1], op=ADD)
+                nc.gpsimd.tensor_tensor(out=out_sb[:, pair], in0=out_sb[:, pair], in1=thirds[:, pair, :, 2], op=ADD)
+            nc.gpsimd.dma_start(out=out_rows[:, group * CHUNK * F : (group + 1) * CHUNK * F], in_=out_sb[:].rearrange("p i j -> p (i j)"))
 
         with tc.manual_schedule():
             for c in range(X_BUFS):

@@ -25,8 +25,13 @@ CHUNK = 4
 GROUPS = ROW_TILES // CHUNK
 CHUNKS = GROUPS * VIEWS
 PAIR = 2
-X_BUFS = 8
+HALVES = CHUNK // PAIR
+PAIRS = CHUNKS * HALVES
+X_BUFS = 6
 T_BANKS = 4
+RUN = 2
+LAG = 3
+SCALE_LAG = LAG + RUN
 
 FLOPS = 2 * B * K * F * 2 * VIEWS
 
@@ -41,10 +46,16 @@ def tile_fusion_r3d_pa_t_kernel(
     x_rows = [x.rearrange("(p t) k -> p (t k)", t=ROW_TILES) for x in xs]
     out_rows = out.rearrange("(p t) j -> p (t j)", t=ROW_TILES)
 
+    def place(pair):
+        chunk, half = divmod(pair, HALVES)
+        group, view = divmod(chunk, VIEWS)
+        return group, view, half
+
     with ExitStack() as ctx:
         const = ctx.enter_context(tc.tile_pool(name="const", bufs=1))
         x_pool = ctx.enter_context(tc.tile_pool(name="x", bufs=X_BUFS))
-        work = ctx.enter_context(tc.tile_pool(name="work", bufs=3))
+        work = ctx.enter_context(tc.tile_pool(name="work", bufs=4))
+        coded = ctx.enter_context(tc.tile_pool(name="coded", bufs=LAG + 2))
         psum_t = ctx.enter_context(tc.psum_pool(name="psum_t", bufs=T_BANKS))
         psum_m = ctx.enter_context(tc.psum_pool(name="psum_m", bufs=8 - T_BANKS))
 
@@ -52,21 +63,24 @@ def tile_fusion_r3d_pa_t_kernel(
         make_identity(nc, identity[:])
 
         x_tiles = {}
+        x_grouped = {}
         x_codes = {}
         x_scales = {}
         w_raw = {}
         w_codes = {}
         w_scales = {}
         products = {}
+        an_sums = {}
         branches = {}
+        averages = {}
 
-        def load_x(c):
-            group, view = divmod(c, VIEWS)
+        def load_x(chunk):
+            group, view = divmod(chunk, VIEWS)
             x_sb = x_pool.tile([P, CHUNK * K], BF16, name="x_sb")
             nc.sync.dma_start(
                 out=x_sb[:], in_=x_rows[view][:, group * CHUNK * K : (group + 1) * CHUNK * K]
             )
-            x_tiles[c] = x_sb
+            x_tiles[chunk] = x_sb
 
         def load_weights(view):
             raw = const.tile([P, 2, 2 * PACK, F], BF16, name="w_raw%d" % view)
@@ -94,16 +108,20 @@ def tile_fusion_r3d_pa_t_kernel(
             w_codes[view] = codes
             w_scales[view] = scales
 
-        def transpose_x(c):
-            x_words = x_tiles.pop(c)[:].bitcast(F32)
-            grouped = work.tile([P, CHUNK * K], BF16, name="x_grouped", align_bytes=64)
+        def transpose(pair):
+            if not 0 <= pair < PAIRS:
+                return
+            chunk, half = divmod(pair, HALVES)
+            x_words = x_tiles[chunk][:].bitcast(F32)
+            grouped = work.tile([P, PAIR * K], BF16, name="x_grouped", align_bytes=64)
             grouped_words = grouped[:].bitcast(F32)
-            for i in range(CHUNK):
+            for i in range(PAIR):
+                first_word = (half * PAIR + i) * WORDS
                 xt = psum_t.tile([P, WORDS], F32, name="xt")
                 for a in range(WORDS // P):
                     nc.tensor.transpose(
                         xt[:, a * P : (a + 1) * P],
-                        x_words[:, i * WORDS + a * P : i * WORDS + (a + 1) * P],
+                        x_words[:, first_word + a * P : first_word + (a + 1) * P],
                         identity[:],
                     )
                 nc.scalar.copy(
@@ -112,85 +130,100 @@ def tile_fusion_r3d_pa_t_kernel(
                     ),
                     in_=xt[:].rearrange("p (g u r) -> p g r u", g=PASSES, u=2),
                 )
-            return grouped
+            x_grouped[pair] = grouped
+            if half == HALVES - 1:
+                x_tiles.pop(chunk)
+                if chunk + X_BUFS < CHUNKS:
+                    load_x(chunk + X_BUFS)
 
-        def quantise_x(c, grouped):
-            codes = work.tile([P, CHUNK * PASSES * P], U32, name="x_codes", align_bytes=64)
-            scales = work.tile([P, CHUNK * PASSES * P], U8, name="x_scales", align_bytes=64)
-            nc.vector.quantize_mx(out=codes[:].bitcast(FP8X4), scales=scales[:], in_=grouped[:])
-            x_codes[c] = codes
-            x_scales[c] = scales
+        def quantise(pair):
+            if not 0 <= pair < PAIRS:
+                return
+            codes = coded.tile([P, PAIR * PASSES * P], U32, name="x_codes", align_bytes=64)
+            scales = coded.tile([P, PAIR * PASSES * P], U8, name="x_scales", align_bytes=64)
+            nc.vector.quantize_mx(out=codes[:].bitcast(FP8X4), scales=scales[:], in_=x_grouped.pop(pair)[:])
+            x_codes[pair] = codes
+            x_scales[pair] = scales
 
-        def multiply(c):
-            view = c % VIEWS
-            codes = x_codes.pop(c)
-            scales = x_scales.pop(c)
-            products[c] = []
-            for h in range(CHUNK // PAIR):
-                acc = psum_m.tile([P, PAIR, 2 * F], F32, name="acc")
-                for i in range(PAIR):
-                    for g in range(PASSES):
-                        rows = slice(((h * PAIR + i) * PASSES + g) * P, ((h * PAIR + i) * PASSES + g + 1) * P)
-                        cols = slice(g * 2 * F, (g + 1) * 2 * F)
-                        nc.tensor.matmul_mx(
-                            out=acc[:, i, :],
-                            lhsT=codes[:, rows].bitcast(FP8X4),
-                            lhsT_scale=scales[:, rows],
-                            rhs=w_codes[view][:, cols].bitcast(FP8X4),
-                            rhs_scale=w_scales[view][:, cols],
-                            start=(g == 0),
-                            stop=(g == PASSES - 1),
-                        )
-                products[c].append(acc)
+        def multiply(pair):
+            if not 0 <= pair < PAIRS:
+                return
+            view = place(pair)[1]
+            codes = x_codes.pop(pair)
+            scales = x_scales.pop(pair)
+            acc = psum_m.tile([P, PAIR, 2 * F], F32, name="acc")
+            for i in range(PAIR):
+                for g in range(PASSES):
+                    rows = slice((i * PASSES + g) * P, (i * PASSES + g + 1) * P)
+                    cols = slice(g * 2 * F, (g + 1) * 2 * F)
+                    nc.tensor.matmul_mx(
+                        out=acc[:, i, :],
+                        lhsT=codes[:, rows].bitcast(FP8X4),
+                        lhsT_scale=scales[:, rows],
+                        rhs=w_codes[view][:, cols].bitcast(FP8X4),
+                        rhs_scale=w_scales[view][:, cols],
+                        start=(g == 0),
+                        stop=(g == PASSES - 1),
+                    )
+            products[pair] = acc
 
-        def scale_branch(c):
-            group, view = divmod(c, VIEWS)
-            if view == 0:
+        def sum_an(pair):
+            if not 0 <= pair < PAIRS:
+                return
+            an_sum = work.tile([P, PAIR], F32, name="an_sum")
+            nc.vector.tensor_reduce(
+                out=an_sum[:], in_=products[pair][:, :, F : 2 * F], axis=mybir.AxisListType.X, op=ADD
+            )
+            an_sums[pair] = an_sum
+
+        def scale(pair):
+            if not 0 <= pair < PAIRS:
+                return
+            group, view, half = place(pair)
+            if view == 0 and half == 0:
                 branches[group] = work.tile([P, CHUNK, VIEWS * F], F32, name="v_sb")
-            v_sb = branches[group]
-            accs = products.pop(c)
-            sums = []
-            for acc in accs:
-                an_sum = work.tile([P, PAIR], F32, name="an_sum", bufs=6)
-                nc.vector.tensor_reduce(out=an_sum[:], in_=acc[:, :, F : 2 * F], axis=mybir.AxisListType.X, op=ADD)
-                sums.append(an_sum)
-            for h, acc in enumerate(accs):
-                nc.vector.scalar_tensor_tensor(
-                    out=v_sb[:, h * PAIR : (h + 1) * PAIR, view * F : (view + 1) * F],
-                    in0=acc[:, :, 0:F],
-                    scalar=1.0 / (F * VIEWS),
-                    in1=sums[h][:].unsqueeze(2).to_broadcast([P, PAIR, F]),
-                    op0=MULT,
-                    op1=MULT,
-                )
+            tiles = slice(half * PAIR, (half + 1) * PAIR)
+            nc.vector.scalar_tensor_tensor(
+                out=branches[group][:, tiles, view * F : (view + 1) * F],
+                in0=products.pop(pair)[:, :, 0:F],
+                scalar=1.0 / (F * VIEWS),
+                in1=an_sums.pop(pair)[:].unsqueeze(2).to_broadcast([P, PAIR, F]),
+                op0=MULT,
+                op1=MULT,
+            )
+            if view == VIEWS - 1:
+                average(group, half)
 
-        def average_and_store(group):
-            v_sb = branches.pop(group)
-            out_sb = work.tile([P, CHUNK, F], F32, name="out_sb")
-            thirds = v_sb[:].rearrange("p i (j s) -> p i j s", s=VIEWS)
-            for h in range(CHUNK // PAIR):
-                pair = slice(h * PAIR, (h + 1) * PAIR)
-                nc.gpsimd.tensor_tensor(out=out_sb[:, pair], in0=thirds[:, pair, :, 0], in1=thirds[:, pair, :, 1], op=ADD)
-                nc.gpsimd.tensor_tensor(out=out_sb[:, pair], in0=out_sb[:, pair], in1=thirds[:, pair, :, 2], op=ADD)
-            nc.gpsimd.dma_start(out=out_rows[:, group * CHUNK * F : (group + 1) * CHUNK * F], in_=out_sb[:].rearrange("p i j -> p (i j)"))
+        def average(group, half):
+            if half == 0:
+                averages[group] = work.tile([P, CHUNK, F], F32, name="out_sb")
+            out_sb = averages[group]
+            thirds = branches[group][:].rearrange("p i (j s) -> p i j s", s=VIEWS)
+            tiles = slice(half * PAIR, (half + 1) * PAIR)
+            nc.gpsimd.tensor_tensor(out=out_sb[:, tiles], in0=thirds[:, tiles, :, 0], in1=thirds[:, tiles, :, 1], op=ADD)
+            nc.gpsimd.tensor_tensor(out=out_sb[:, tiles], in0=out_sb[:, tiles], in1=thirds[:, tiles, :, 2], op=ADD)
+            if half == HALVES - 1:
+                nc.sync.dma_start(
+                    out=out_rows[:, group * CHUNK * F : (group + 1) * CHUNK * F],
+                    in_=out_sb[:].rearrange("p i j -> p (i j)"),
+                )
+                branches.pop(group)
+                averages.pop(group)
 
         with tc.manual_schedule():
-            for c in range(X_BUFS):
-                load_x(c)
-                if c < VIEWS:
-                    load_weights(c)
-            grouped = {}
-            for s in range(CHUNKS + 2):
-                if s < CHUNKS:
-                    grouped[s] = transpose_x(s)
-                    if s + X_BUFS < CHUNKS:
-                        load_x(s + X_BUFS)
-                if s < VIEWS:
-                    quantise_weights(s)
-                if 1 <= s <= CHUNKS:
-                    quantise_x(s - 1, grouped.pop(s - 1))
-                    multiply(s - 1)
-                if s >= 2:
-                    scale_branch(s - 2)
-                    if (s - 2) % VIEWS == VIEWS - 1:
-                        average_and_store((s - 2) // VIEWS)
+            for chunk in range(X_BUFS):
+                load_x(chunk)
+                if chunk < VIEWS:
+                    load_weights(chunk)
+            for first in range(0, PAIRS + SCALE_LAG, RUN):
+                run = range(first, first + RUN)
+                for pair in run:
+                    transpose(pair)
+                for pair in run:
+                    sum_an(pair - SCALE_LAG)
+                    quantise(pair - 1)
+                    if pair % HALVES == 1 and pair // HALVES < VIEWS:
+                        quantise_weights(pair // HALVES)
+                    scale(pair - SCALE_LAG)
+                for pair in run:
+                    multiply(pair - LAG)

@@ -29,7 +29,7 @@ HALVES = CHUNK // PAIR
 PAIRS = CHUNKS * HALVES
 X_BUFS = 6
 T_BANKS = 4
-RUN = 2
+RUN = 1
 LAG = 3
 SCALE_LAG = LAG + RUN
 

@@ -33,6 +33,10 @@ RUN = 1
 LAG = 3
 SCALE_LAG = LAG + RUN
 
+WHOLE = 42
+FIRST_TRIPLE = (0, 1, 2)
+EDGES = (slice(126, 128), slice(0, 128, 127), slice(0, 2))
+
 FLOPS = 2 * B * K * F * 2 * VIEWS
 
 
@@ -71,8 +75,9 @@ def tile_fusion_r3d_pa_t_kernel(
         w_scales = {}
         products = {}
         an_sums = {}
-        branches = {}
-        averages = {}
+        triples = {}
+        edges = {}
+        outs = {}
 
         def load_x(chunk):
             group, view = divmod(chunk, VIEWS)
@@ -170,52 +175,84 @@ def tile_fusion_r3d_pa_t_kernel(
         def sum_an(pair):
             if not 0 <= pair < PAIRS:
                 return
-            an_sum = work.tile([P, PAIR], F32, name="an_sum")
+            group, view, half = place(pair)
+            if view == 0 and half == 0:
+                an_sums[group] = work.tile([P, VIEWS, CHUNK], F32, name="an_sum")
             nc.vector.tensor_reduce(
-                out=an_sum[:], in_=products[pair][:, :, F : 2 * F], axis=mybir.AxisListType.X, op=ADD
+                out=an_sums[group][:, view, half * PAIR : (half + 1) * PAIR],
+                in_=products[pair][:, :, F : 2 * F],
+                axis=mybir.AxisListType.X,
+                op=ADD,
             )
-            an_sums[pair] = an_sum
+
+        def sum_triples(pair):
+            if not 0 <= pair < PAIRS:
+                return
+            group, view, half = place(pair)
+            if half == 0:
+                triples[group, view] = work.tile([P, CHUNK, WHOLE], F32, name="triple_sums")
+            first = FIRST_TRIPLE[view]
+            nc.vector.tensor_reduce(
+                out=triples[group, view][:, half * PAIR : (half + 1) * PAIR, :],
+                in_=products[pair][:, :, first : first + 3 * WHOLE].rearrange("p i (j s) -> p i j s", s=VIEWS),
+                axis=mybir.AxisListType.X,
+                op=ADD,
+            )
+
+        def scale_edges(pair):
+            if not 0 <= pair < PAIRS:
+                return
+            group, view, half = place(pair)
+            if view == 0 and half == 0:
+                edges[group] = work.tile([P, CHUNK, VIEWS * 2], F32, name="edge_sb")
+            tiles = slice(half * PAIR, (half + 1) * PAIR)
+            nc.vector.scalar_tensor_tensor(
+                out=edges[group][:, tiles, 2 * view : 2 * view + 2],
+                in0=products.pop(pair)[:, :, EDGES[view]],
+                scalar=1.0 / (F * VIEWS),
+                in1=an_sums[group][:, view, tiles].unsqueeze(2).to_broadcast([P, PAIR, 2]),
+                op0=MULT,
+                op1=MULT,
+            )
 
         def scale(pair):
             if not 0 <= pair < PAIRS:
                 return
             group, view, half = place(pair)
-            if view == 0 and half == 0:
-                branches[group] = work.tile([P, CHUNK, VIEWS * F], F32, name="v_sb")
-            tiles = slice(half * PAIR, (half + 1) * PAIR)
+            if half != HALVES - 1:
+                return
+            if view == 0:
+                outs[group] = work.tile([P, CHUNK, F], F32, name="out_sb")
+            out_sb = outs[group]
+            first = (WHOLE + 1) * view
             nc.vector.scalar_tensor_tensor(
-                out=branches[group][:, tiles, view * F : (view + 1) * F],
-                in0=products.pop(pair)[:, :, 0:F],
+                out=out_sb[:, :, first : first + WHOLE],
+                in0=triples.pop((group, view))[:],
                 scalar=1.0 / (F * VIEWS),
-                in1=an_sums.pop(pair)[:].unsqueeze(2).to_broadcast([P, PAIR, F]),
+                in1=an_sums[group][:, view, :].unsqueeze(2).to_broadcast([P, CHUNK, WHOLE]),
                 op0=MULT,
                 op1=MULT,
             )
             if view == VIEWS - 1:
-                average(group, half)
-
-        def average(group, half):
-            if half == 0:
-                averages[group] = work.tile([P, CHUNK, F], F32, name="out_sb")
-            out_sb = averages[group]
-            thirds = branches[group][:].rearrange("p i (j s) -> p i j s", s=VIEWS)
-            tiles = slice(half * PAIR, (half + 1) * PAIR)
-            nc.gpsimd.tensor_tensor(out=out_sb[:, tiles], in0=thirds[:, tiles, :, 0], in1=thirds[:, tiles, :, 1], op=ADD)
-            nc.gpsimd.tensor_tensor(out=out_sb[:, tiles], in0=out_sb[:, tiles], in1=thirds[:, tiles, :, 2], op=ADD)
-            if half == HALVES - 1:
+                nc.vector.tensor_reduce(
+                    out=out_sb[:, :, WHOLE : 2 * WHOLE + 2 : WHOLE + 1],
+                    in_=edges.pop(group)[:].rearrange("p i (j s) -> p i j s", s=VIEWS),
+                    axis=mybir.AxisListType.X,
+                    op=ADD,
+                )
                 nc.sync.dma_start(
                     out=out_rows[:, group * CHUNK * F : (group + 1) * CHUNK * F],
                     in_=out_sb[:].rearrange("p i j -> p (i j)"),
                 )
-                branches.pop(group)
-                averages.pop(group)
+                outs.pop(group)
+                an_sums.pop(group)
 
         with tc.manual_schedule():
             for chunk in range(X_BUFS):
                 load_x(chunk)
                 if chunk < VIEWS:
                     load_weights(chunk)
-            for first in range(0, PAIRS + SCALE_LAG, RUN):
+            for first in range(0, PAIRS + SCALE_LAG + 1, RUN):
                 run = range(first, first + RUN)
                 for pair in run:
                     transpose(pair)
@@ -224,6 +261,8 @@ def tile_fusion_r3d_pa_t_kernel(
                     quantise(pair - 1)
                     if pair % HALVES == 1 and pair // HALVES < VIEWS:
                         quantise_weights(pair // HALVES)
-                    scale(pair - SCALE_LAG)
+                    sum_triples(pair - SCALE_LAG)
+                    scale_edges(pair - SCALE_LAG)
+                    scale(pair - SCALE_LAG - 1)
                 for pair in run:
                     multiply(pair - LAG)

@@ -27,7 +27,8 @@ CHUNKS = GROUPS * VIEWS
 PAIR = 2
 HALVES = CHUNK // PAIR
 PAIRS = CHUNKS * HALVES
-X_BUFS = 6
+VIEW_PAIRS = GROUPS * HALVES
+X_BUFS = 8
 T_BANKS = 4
 RUN = 1
 LAG = 3
@@ -52,7 +53,7 @@ def tile_fusion_r3d_pa_t_kernel(
 
     def place(pair):
         chunk, half = divmod(pair, HALVES)
-        group, view = divmod(chunk, VIEWS)
+        view, group = divmod(chunk, GROUPS)
         return group, view, half
 
     with ExitStack() as ctx:
@@ -65,26 +66,31 @@ def tile_fusion_r3d_pa_t_kernel(
 
         identity = const.tile([P, P], F32)
         make_identity(nc, identity[:])
+        out_sb = const.tile([P, ROW_TILES, F], F32)
+        edge_sb = const.tile([P, ROW_TILES, VIEWS * 2], F32)
 
         x_tiles = {}
         x_grouped = {}
         x_codes = {}
         x_scales = {}
         w_raw = {}
+        w_grouped = {}
         w_codes = {}
         w_scales = {}
         products = {}
         an_sums = {}
         triples = {}
-        edges = {}
-        outs = {}
 
-        def load_x(chunk):
-            group, view = divmod(chunk, VIEWS)
+        def load_x(chunk, pieces=1):
+            view, group = divmod(chunk, GROUPS)
             x_sb = x_pool.tile([P, CHUNK * K], BF16, name="x_sb")
-            nc.sync.dma_start(
-                out=x_sb[:], in_=x_rows[view][:, group * CHUNK * K : (group + 1) * CHUNK * K]
-            )
+            width = CHUNK * K // pieces
+            for piece in range(pieces):
+                first = group * CHUNK * K + piece * width
+                nc.sync.dma_start(
+                    out=x_sb[:, piece * width : (piece + 1) * width],
+                    in_=x_rows[view][:, first : first + width],
+                )
             x_tiles[chunk] = x_sb
 
         def load_weights(view):
@@ -96,19 +102,23 @@ def tile_fusion_r3d_pa_t_kernel(
                 )
             w_raw[view] = raw
 
-        def quantise_weights(view):
-            grouped = const.tile([P, PASSES, 2, F, PACK], BF16, name="w_grouped%d" % view, align_bytes=64)
-            for g in range(PASSES):
-                nc.vector.tensor_copy(
-                    out=grouped[:, g],
-                    in_=w_raw[view][:, :, g * PACK : (g + 1) * PACK, :].rearrange("p w t f -> p w f t"),
+        def group_weights(view, g):
+            if g == 0:
+                w_grouped[view] = const.tile(
+                    [P, PASSES, 2, F, PACK], BF16, name="w_grouped%d" % view, align_bytes=64
                 )
+            nc.vector.tensor_copy(
+                out=w_grouped[view][:, g],
+                in_=w_raw[view][:, :, g * PACK : (g + 1) * PACK, :].rearrange("p w t f -> p w f t"),
+            )
+
+        def quantise_weights(view):
             codes = const.tile([P, PASSES * 2 * F], U32, name="w_codes%d" % view, align_bytes=64)
             scales = const.tile([P, PASSES * 2 * F], U8, name="w_scales%d" % view, align_bytes=64)
             nc.vector.quantize_mx(
                 out=codes[:].bitcast(FP8X4),
                 scales=scales[:],
-                in_=grouped[:].rearrange("p g w f t -> p (g w f t)"),
+                in_=w_grouped[view][:].rearrange("p g w f t -> p (g w f t)"),
             )
             w_codes[view] = codes
             w_scales[view] = scales
@@ -176,10 +186,10 @@ def tile_fusion_r3d_pa_t_kernel(
             if not 0 <= pair < PAIRS:
                 return
             group, view, half = place(pair)
-            if view == 0 and half == 0:
-                an_sums[group] = work.tile([P, VIEWS, CHUNK], F32, name="an_sum")
+            if half == 0:
+                an_sums[group, view] = work.tile([P, CHUNK], F32, name="an_sum")
             nc.vector.tensor_reduce(
-                out=an_sums[group][:, view, half * PAIR : (half + 1) * PAIR],
+                out=an_sums[group, view][:, half * PAIR : (half + 1) * PAIR],
                 in_=products[pair][:, :, F : 2 * F],
                 axis=mybir.AxisListType.X,
                 op=ADD,
@@ -203,14 +213,13 @@ def tile_fusion_r3d_pa_t_kernel(
             if not 0 <= pair < PAIRS:
                 return
             group, view, half = place(pair)
-            if view == 0 and half == 0:
-                edges[group] = work.tile([P, CHUNK, VIEWS * 2], F32, name="edge_sb")
             tiles = slice(half * PAIR, (half + 1) * PAIR)
+            first = group * CHUNK + half * PAIR
             nc.vector.scalar_tensor_tensor(
-                out=edges[group][:, tiles, 2 * view : 2 * view + 2],
+                out=edge_sb[:, first : first + PAIR, 2 * view : 2 * view + 2],
                 in0=products.pop(pair)[:, :, EDGES[view]],
                 scalar=1.0 / (F * VIEWS),
-                in1=an_sums[group][:, view, tiles].unsqueeze(2).to_broadcast([P, PAIR, 2]),
+                in1=an_sums[group, view][:, tiles].unsqueeze(2).to_broadcast([P, PAIR, 2]),
                 op0=MULT,
                 op1=MULT,
             )
@@ -221,37 +230,35 @@ def tile_fusion_r3d_pa_t_kernel(
             group, view, half = place(pair)
             if half != HALVES - 1:
                 return
-            if view == 0:
-                outs[group] = work.tile([P, CHUNK, F], F32, name="out_sb")
-            out_sb = outs[group]
+            tiles = slice(group * CHUNK, (group + 1) * CHUNK)
             first = (WHOLE + 1) * view
             nc.vector.scalar_tensor_tensor(
-                out=out_sb[:, :, first : first + WHOLE],
+                out=out_sb[:, tiles, first : first + WHOLE],
                 in0=triples.pop((group, view))[:],
                 scalar=1.0 / (F * VIEWS),
-                in1=an_sums[group][:, view, :].unsqueeze(2).to_broadcast([P, CHUNK, WHOLE]),
+                in1=an_sums.pop((group, view))[:].unsqueeze(2).to_broadcast([P, CHUNK, WHOLE]),
                 op0=MULT,
                 op1=MULT,
             )
             if view == VIEWS - 1:
                 nc.vector.tensor_reduce(
-                    out=out_sb[:, :, WHOLE : 2 * WHOLE + 2 : WHOLE + 1],
-                    in_=edges.pop(group)[:].rearrange("p i (j s) -> p i j s", s=VIEWS),
+                    out=out_sb[:, tiles, WHOLE : 2 * WHOLE + 2 : WHOLE + 1],
+                    in_=edge_sb[:, tiles].rearrange("p i (j s) -> p i j s", s=VIEWS),
                     axis=mybir.AxisListType.X,
                     op=ADD,
                 )
                 nc.sync.dma_start(
                     out=out_rows[:, group * CHUNK * F : (group + 1) * CHUNK * F],
-                    in_=out_sb[:].rearrange("p i j -> p (i j)"),
+                    in_=out_sb[:, tiles].rearrange("p i j -> p (i j)"),
                 )
-                outs.pop(group)
-                an_sums.pop(group)
 
         with tc.manual_schedule():
             for chunk in range(X_BUFS):
-                load_x(chunk)
-                if chunk < VIEWS:
-                    load_weights(chunk)
+                load_x(chunk, pieces=CHUNK if chunk < 2 else 1)
+                if chunk == 0:
+                    load_weights(0)
+            for view in range(1, VIEWS):
+                load_weights(view)
             for first in range(0, PAIRS + SCALE_LAG + 1, RUN):
                 run = range(first, first + RUN)
                 for pair in run:
@@ -259,8 +266,16 @@ def tile_fusion_r3d_pa_t_kernel(
                 for pair in run:
                     sum_an(pair - SCALE_LAG)
                     quantise(pair - 1)
-                    if pair % HALVES == 1 and pair // HALVES < VIEWS:
-                        quantise_weights(pair // HALVES)
+                    if pair == 1:
+                        for g in range(PASSES):
+                            group_weights(0, g)
+                        quantise_weights(0)
+                    view, step = divmod(pair + PASSES + 1, VIEW_PAIRS)
+                    if 0 < view < VIEWS and step <= PASSES:
+                        if step < PASSES:
+                            group_weights(view, step)
+                        else:
+                            quantise_weights(view)
                     sum_triples(pair - SCALE_LAG)
                     scale_edges(pair - SCALE_LAG)
                     scale(pair - SCALE_LAG - 1)

@@ -28,6 +28,7 @@ PAIR = 2
 HALVES = CHUNK // PAIR
 PAIRS = CHUNKS * HALVES
 VIEW_PAIRS = GROUPS * HALVES
+SCALAR_SHARE = 3
 X_BUFS = 8
 T_BANKS = 4
 RUN = 1
@@ -188,6 +189,16 @@ def tile_fusion_r3d_pa_t_kernel(
             group, view, half = place(pair)
             if half == 0:
                 an_sums[group, view] = work.tile([P, CHUNK], F32, name="an_sum")
+            if pair % SCALAR_SHARE == 0:
+                for i in range(PAIR):
+                    an_copy = work.tile([P, F], BF16, name="an_copy")
+                    nc.scalar.activation(
+                        out=an_copy[:],
+                        in_=products[pair][:, i, F : 2 * F],
+                        func=mybir.ActivationFunctionType.Copy,
+                        accum_out=an_sums[group, view][:, half * PAIR + i : half * PAIR + i + 1],
+                    )
+                return
             nc.vector.tensor_reduce(
                 out=an_sums[group, view][:, half * PAIR : (half + 1) * PAIR],
                 in_=products[pair][:, :, F : 2 * F],

@@ -183,13 +183,13 @@ def tile_fusion_r3d_pa_t_kernel(
                     )
             products[pair] = acc
 
-        def sum_an(pair):
-            if not 0 <= pair < PAIRS:
+        def sum_an(pair, on_scalar):
+            if not 0 <= pair < PAIRS or on_scalar != (pair % SCALAR_SHARE == 0):
                 return
             group, view, half = place(pair)
-            if half == 0:
+            if (group, view) not in an_sums:
                 an_sums[group, view] = work.tile([P, CHUNK], F32, name="an_sum")
-            if pair % SCALAR_SHARE == 0:
+            if on_scalar:
                 for i in range(PAIR):
                     an_copy = work.tile([P, F], BF16, name="an_copy")
                     nc.scalar.activation(
@@ -273,9 +273,11 @@ def tile_fusion_r3d_pa_t_kernel(
             for first in range(0, PAIRS + SCALE_LAG + 1, RUN):
                 run = range(first, first + RUN)
                 for pair in run:
+                    sum_an(pair - SCALE_LAG, on_scalar=True)
+                for pair in run:
                     transpose(pair)
                 for pair in run:
-                    sum_an(pair - SCALE_LAG)
+                    sum_an(pair - SCALE_LAG, on_scalar=False)
                     quantise(pair - 1)
                     if pair == 1:
                         for g in range(PASSES):

@@ -29,6 +29,8 @@ HALVES = CHUNK // PAIR
 PAIRS = CHUNKS * HALVES
 VIEW_PAIRS = GROUPS * HALVES
 SCALAR_SHARE = 3
+SCALAR_TAIL = 4
+NEIGHBOURS = 4
 X_BUFS = 8
 T_BANKS = 4
 RUN = 1
@@ -109,8 +111,10 @@ def tile_fusion_r3d_pa_t_kernel(
                     [P, PASSES, 2, F, PACK], BF16, name="w_grouped%d" % view, align_bytes=64
                 )
             nc.vector.tensor_copy(
-                out=w_grouped[view][:, g],
-                in_=w_raw[view][:, :, g * PACK : (g + 1) * PACK, :].rearrange("p w t f -> p w f t"),
+                out=w_grouped[view][:, g].rearrange("p w (c i) t -> p w c t i", i=NEIGHBOURS),
+                in_=w_raw[view][:, :, g * PACK : (g + 1) * PACK, :].rearrange(
+                    "p w t (c i) -> p w c t i", i=NEIGHBOURS
+                ),
             )
 
         def quantise_weights(view):
@@ -184,7 +188,7 @@ def tile_fusion_r3d_pa_t_kernel(
             products[pair] = acc
 
         def sum_an(pair, on_scalar):
-            if not 0 <= pair < PAIRS or on_scalar != (pair % SCALAR_SHARE == 0):
+            if not 0 <= pair < PAIRS or on_scalar != (pair % SCALAR_SHARE == 0 or pair >= PAIRS - SCALAR_TAIL):
                 return
             group, view, half = place(pair)
             if (group, view) not in an_sums:

@@ -28,12 +28,12 @@ PAIR = 2
 HALVES = CHUNK // PAIR
 PAIRS = CHUNKS * HALVES
 VIEW_PAIRS = GROUPS * HALVES
-SCALAR_SHARE = 3
+SCALAR_SHARE = 2
 SCALAR_TAIL = 4
 NEIGHBOURS = 4
 X_BUFS = 8
 T_BANKS = 4
-RUN = 1
+RUN = 2
 LAG = 3
 SCALE_LAG = LAG + RUN
 
@@ -62,7 +62,7 @@ def tile_fusion_r3d_pa_t_kernel(
     with ExitStack() as ctx:
         const = ctx.enter_context(tc.tile_pool(name="const", bufs=1))
         x_pool = ctx.enter_context(tc.tile_pool(name="x", bufs=X_BUFS))
-        work = ctx.enter_context(tc.tile_pool(name="work", bufs=4))
+        work = ctx.enter_context(tc.tile_pool(name="work", bufs=6))
         coded = ctx.enter_context(tc.tile_pool(name="coded", bufs=LAG + 2))
         psum_t = ctx.enter_context(tc.psum_pool(name="psum_t", bufs=T_BANKS))
         psum_m = ctx.enter_context(tc.psum_pool(name="psum_m", bufs=8 - T_BANKS))
@@ -84,7 +84,7 @@ def tile_fusion_r3d_pa_t_kernel(
         an_sums = {}
         triples = {}
 
-        def load_x(chunk, pieces=1):
+        def load_x(chunk, pieces=1, weights_after=None):
             view, group = divmod(chunk, GROUPS)
             x_sb = x_pool.tile([P, CHUNK * K], BF16, name="x_sb")
             width = CHUNK * K // pieces
@@ -94,6 +94,8 @@ def tile_fusion_r3d_pa_t_kernel(
                     out=x_sb[:, piece * width : (piece + 1) * width],
                     in_=x_rows[view][:, first : first + width],
                 )
+                if piece == weights_after:
+                    load_weights(view)
             x_tiles[chunk] = x_sb
 
         def load_weights(view):
@@ -269,9 +271,7 @@ def tile_fusion_r3d_pa_t_kernel(
 
         with tc.manual_schedule():
             for chunk in range(X_BUFS):
-                load_x(chunk, pieces=CHUNK if chunk < 2 else 1)
-                if chunk == 0:
-                    load_weights(0)
+                load_x(chunk, pieces=CHUNK if chunk < 3 else 1, weights_after=1 if chunk == 0 else None)
             for view in range(1, VIEWS):
                 load_weights(view)
             for first in range(0, PAIRS + SCALE_LAG + 1, RUN):
@@ -282,8 +282,8 @@ def tile_fusion_r3d_pa_t_kernel(
                     transpose(pair)
                 for pair in run:
                     sum_an(pair - SCALE_LAG, on_scalar=False)
-                    quantise(pair - 1)
-                    if pair == 1:
+                    quantise(pair - RUN)
+                    if pair == RUN - 1:
                         for g in range(PASSES):
                             group_weights(0, g)
                         quantise_weights(0)

@@ -31,6 +31,7 @@ VIEW_PAIRS = GROUPS * HALVES
 SCALAR_SHARE = 2
 SCALAR_TAIL = 4
 NEIGHBOURS = 4
+HALFWAY = 4
 X_BUFS = 8
 T_BANKS = 4
 RUN = 2
@@ -40,6 +41,10 @@ SCALE_LAG = LAG + RUN
 WHOLE = 42
 FIRST_TRIPLE = (0, 1, 2)
 EDGES = (slice(126, 128), slice(0, 128, 127), slice(0, 2))
+
+def span(view):
+    return 1 if view == VIEWS - 1 else 2
+
 
 FLOPS = 2 * B * K * F * 2 * VIEWS
 
@@ -157,6 +162,8 @@ def tile_fusion_r3d_pa_t_kernel(
                 x_tiles.pop(chunk)
                 if chunk + X_BUFS < CHUNKS:
                     load_x(chunk + X_BUFS)
+                if chunk == HALFWAY:
+                    load_weights(2)
 
         def quantise(pair):
             if not 0 <= pair < PAIRS:
@@ -193,8 +200,10 @@ def tile_fusion_r3d_pa_t_kernel(
             if not 0 <= pair < PAIRS or on_scalar != (pair % SCALAR_SHARE == 0 or pair >= PAIRS - SCALAR_TAIL):
                 return
             group, view, half = place(pair)
-            if (group, view) not in an_sums:
-                an_sums[group, view] = work.tile([P, CHUNK], F32, name="an_sum")
+            block, member = divmod(group, span(view))
+            if (block, view) not in an_sums:
+                an_sums[block, view] = work.tile([P, span(view) * CHUNK], F32, name="an_sum_%d" % span(view))
+            first = member * CHUNK + half * PAIR
             if on_scalar:
                 for i in range(PAIR):
                     an_copy = work.tile([P, F], BF16, name="an_copy")
@@ -202,11 +211,11 @@ def tile_fusion_r3d_pa_t_kernel(
                         out=an_copy[:],
                         in_=products[pair][:, i, F : 2 * F],
                         func=mybir.ActivationFunctionType.Copy,
-                        accum_out=an_sums[group, view][:, half * PAIR + i : half * PAIR + i + 1],
+                        accum_out=an_sums[block, view][:, first + i : first + i + 1],
                     )
                 return
             nc.vector.tensor_reduce(
-                out=an_sums[group, view][:, half * PAIR : (half + 1) * PAIR],
+                out=an_sums[block, view][:, first : first + PAIR],
                 in_=products[pair][:, :, F : 2 * F],
                 axis=mybir.AxisListType.X,
                 op=ADD,
@@ -216,11 +225,15 @@ def tile_fusion_r3d_pa_t_kernel(
             if not 0 <= pair < PAIRS:
                 return
             group, view, half = place(pair)
-            if half == 0:
-                triples[group, view] = work.tile([P, CHUNK, WHOLE], F32, name="triple_sums")
+            block, member = divmod(group, span(view))
+            if member == 0 and half == 0:
+                triples[block, view] = work.tile(
+                    [P, span(view) * CHUNK, WHOLE], F32, name="triple_sums_%d" % span(view)
+                )
+            tile = member * CHUNK + half * PAIR
             first = FIRST_TRIPLE[view]
             nc.vector.tensor_reduce(
-                out=triples[group, view][:, half * PAIR : (half + 1) * PAIR, :],
+                out=triples[block, view][:, tile : tile + PAIR, :],
                 in_=products[pair][:, :, first : first + 3 * WHOLE].rearrange("p i (j s) -> p i j s", s=VIEWS),
                 axis=mybir.AxisListType.X,
                 op=ADD,
@@ -230,13 +243,14 @@ def tile_fusion_r3d_pa_t_kernel(
             if not 0 <= pair < PAIRS:
                 return
             group, view, half = place(pair)
-            tiles = slice(half * PAIR, (half + 1) * PAIR)
+            block, member = divmod(group, span(view))
+            tile = member * CHUNK + half * PAIR
             first = group * CHUNK + half * PAIR
             nc.vector.scalar_tensor_tensor(
                 out=edge_sb[:, first : first + PAIR, 2 * view : 2 * view + 2],
                 in0=products.pop(pair)[:, :, EDGES[view]],
                 scalar=1.0 / (F * VIEWS),
-                in1=an_sums[group, view][:, tiles].unsqueeze(2).to_broadcast([P, PAIR, 2]),
+                in1=an_sums[block, view][:, tile : tile + PAIR].unsqueeze(2).to_broadcast([P, PAIR, 2]),
                 op0=MULT,
                 op1=MULT,
             )
@@ -245,15 +259,17 @@ def tile_fusion_r3d_pa_t_kernel(
             if not 0 <= pair < PAIRS:
                 return
             group, view, half = place(pair)
-            if half != HALVES - 1:
+            block, member = divmod(group, span(view))
+            if half != HALVES - 1 or member != span(view) - 1:
                 return
-            tiles = slice(group * CHUNK, (group + 1) * CHUNK)
+            count = span(view) * CHUNK
+            tiles = slice(block * count, (block + 1) * count)
             first = (WHOLE + 1) * view
             nc.vector.scalar_tensor_tensor(
                 out=out_sb[:, tiles, first : first + WHOLE],
-                in0=triples.pop((group, view))[:],
+                in0=triples.pop((block, view))[:],
                 scalar=1.0 / (F * VIEWS),
-                in1=an_sums.pop((group, view))[:].unsqueeze(2).to_broadcast([P, CHUNK, WHOLE]),
+                in1=an_sums.pop((block, view))[:].unsqueeze(2).to_broadcast([P, count, WHOLE]),
                 op0=MULT,
                 op1=MULT,
             )
@@ -271,9 +287,8 @@ def tile_fusion_r3d_pa_t_kernel(
 
         with tc.manual_schedule():
             for chunk in range(X_BUFS):
-                load_x(chunk, pieces=CHUNK if chunk < 3 else 1, weights_after=1 if chunk == 0 else None)
-            for view in range(1, VIEWS):
-                load_weights(view)
+                load_x(chunk, pieces=CHUNK if chunk == 0 else HALVES, weights_after=1 if chunk == 0 else None)
+            load_weights(1)
             for first in range(0, PAIRS + SCALE_LAG + 1, RUN):
                 run = range(first, first + RUN)
                 for pair in run:
@@ -287,7 +302,7 @@ def tile_fusion_r3d_pa_t_kernel(
                         for g in range(PASSES):
                             group_weights(0, g)
                         quantise_weights(0)
-                    view, step = divmod(pair + PASSES + 1, VIEW_PAIRS)
+                    view, step = divmod(pair + 1, VIEW_PAIRS)
                     if 0 < view < VIEWS and step <= PASSES:
                         if step < PASSES:
                             group_weights(view, step)

from contextlib import ExitStack

import concourse.mybir as mybir
from concourse.masks import make_identity

F32 = mybir.dt.float32
BF16 = mybir.dt.bfloat16
U32 = mybir.dt.uint32
U8 = mybir.dt.uint8
FP8X4 = mybir.dt.float8_e4m3fn_x4
ADD = mybir.AluOpType.add
MULT = mybir.AluOpType.mult

P = 128
B = 4096
K = 1024
F = 128
VIEWS = 3
PACK = 4
K_PASS = P * PACK
PASSES = K // K_PASS
WORDS = K // 2
ROW_TILES = B // P
CHUNK = 4
GROUPS = ROW_TILES // CHUNK
CHUNKS = GROUPS * VIEWS
PAIR = 2
HALVES = CHUNK // PAIR
PAIRS = CHUNKS * HALVES
VIEW_PAIRS = GROUPS * HALVES
SCALAR_SHARE = 2
SCALAR_TAIL = 4
NEIGHBOURS = 4
HALFWAY = 4
X_BUFS = 8
T_BANKS = 4
RUN = 2
LAG = 3
SCALE_LAG = LAG + RUN

WHOLE = 42
FIRST_TRIPLE = (0, 1, 2)
EDGES = (slice(126, 128), slice(0, 128, 127), slice(0, 2))

def span(view):
    return 1 if view == VIEWS - 1 else 2


FLOPS = 2 * B * K * F * 2 * VIEWS


def tile_fusion_r3d_pa_t_kernel(
    tc, x_dash, x_rear, x_right, Wd_nm, Wd_an, Wr_nm, Wr_an, Wt_nm, Wt_an, out
):
    nc = tc.nc
    xs = (x_dash, x_rear, x_right)
    weights = ((Wd_nm, Wd_an), (Wr_nm, Wr_an), (Wt_nm, Wt_an))

    x_rows = [x.rearrange("(p t) k -> p (t k)", t=ROW_TILES) for x in xs]
    out_rows = out.rearrange("(p t) j -> p (t j)", t=ROW_TILES)

    def place(pair):
        chunk, half = divmod(pair, HALVES)
        view, group = divmod(chunk, GROUPS)
        return group, view, half

    with ExitStack() as ctx:
        const = ctx.enter_context(tc.tile_pool(name="const", bufs=1))
        x_pool = ctx.enter_context(tc.tile_pool(name="x", bufs=X_BUFS))
        work = ctx.enter_context(tc.tile_pool(name="work", bufs=6))
        coded = ctx.enter_context(tc.tile_pool(name="coded", bufs=LAG + 2))
        psum_t = ctx.enter_context(tc.psum_pool(name="psum_t", bufs=T_BANKS))
        psum_m = ctx.enter_context(tc.psum_pool(name="psum_m", bufs=8 - T_BANKS))

        identity = const.tile([P, P], F32)
        make_identity(nc, identity[:])
        out_sb = const.tile([P, ROW_TILES, F], F32)
        edge_sb = const.tile([P, ROW_TILES, VIEWS * 2], F32)

        x_tiles = {}
        x_grouped = {}
        x_codes = {}
        x_scales = {}
        w_raw = {}
        w_grouped = {}
        w_codes = {}
        w_scales = {}
        products = {}
        an_sums = {}
        triples = {}

        def load_x(chunk, pieces=1, weights_after=None):
            view, group = divmod(chunk, GROUPS)
            x_sb = x_pool.tile([P, CHUNK * K], BF16, name="x_sb")
            width = CHUNK * K // pieces
            for piece in range(pieces):
                first = group * CHUNK * K + piece * width
                nc.sync.dma_start(
                    out=x_sb[:, piece * width : (piece + 1) * width],
                    in_=x_rows[view][:, first : first + width],
                )
                if piece == weights_after:
                    load_weights(view)
            x_tiles[chunk] = x_sb

        def load_weights(view):
            raw = const.tile([P, 2, 2 * PACK, F], BF16, name="w_raw%d" % view)
            for w in range(2):
                nc.sync.dma_start(
                    out=raw[:, w].rearrange("p (a e) f -> p a (e f)", e=2),
                    in_=weights[view][w].rearrange("(a p e) f -> p a (e f)", p=P, e=2),
                )
            w_raw[view] = raw

        def group_weights(view, g):
            if g == 0:
                w_grouped[view] = const.tile(
                    [P, PASSES, 2, F, PACK], BF16, name="w_grouped%d" % view, align_bytes=64
                )
            nc.vector.tensor_copy(
                out=w_grouped[view][:, g].rearrange("p w (c i) t -> p w c t i", i=NEIGHBOURS),
                in_=w_raw[view][:, :, g * PACK : (g + 1) * PACK, :].rearrange(
                    "p w t (c i) -> p w c t i", i=NEIGHBOURS
                ),
            )

        def quantise_weights(view):
            codes = const.tile([P, PASSES * 2 * F], U32, name="w_codes%d" % view, align_bytes=64)
            scales = const.tile([P, PASSES * 2 * F], U8, name="w_scales%d" % view, align_bytes=64)
            nc.vector.quantize_mx(
                out=codes[:].bitcast(FP8X4),
                scales=scales[:],
                in_=w_grouped[view][:].rearrange("p g w f t -> p (g w f t)"),
            )
            w_codes[view] = codes
            w_scales[view] = scales

        def transpose(pair):
            if not 0 <= pair < PAIRS:
                return
            chunk, half = divmod(pair, HALVES)
            x_words = x_tiles[chunk][:].bitcast(F32)
            grouped = work.tile([P, PAIR * K], BF16, name="x_grouped", align_bytes=64)
            grouped_words = grouped[:].bitcast(F32)
            for i in range(PAIR):
                first_word = (half * PAIR + i) * WORDS
                xt = psum_t.tile([P, WORDS], F32, name="xt")
                for a in range(WORDS // P):
                    nc.tensor.transpose(
                        xt[:, a * P : (a + 1) * P],
                        x_words[:, first_word + a * P : first_word + (a + 1) * P],
                        identity[:],
                    )
                nc.scalar.copy(
                    out=grouped_words[:, i * WORDS : (i + 1) * WORDS].rearrange(
                        "p (g r u) -> p g r u", g=PASSES, u=2
                    ),
                    in_=xt[:].rearrange("p (g u r) -> p g r u", g=PASSES, u=2),
                )
            x_grouped[pair] = grouped
            if half == HALVES - 1:
                x_tiles.pop(chunk)
                if chunk + X_BUFS < CHUNKS:
                    load_x(chunk + X_BUFS)
                if chunk == HALFWAY:
                    load_weights(2)

        def quantise(pair):
            if not 0 <= pair < PAIRS:
                return
            codes = coded.tile([P, PAIR * PASSES * P], U32, name="x_codes", align_bytes=64)
            scales = coded.tile([P, PAIR * PASSES * P], U8, name="x_scales", align_bytes=64)
            nc.vector.quantize_mx(out=codes[:].bitcast(FP8X4), scales=scales[:], in_=x_grouped.pop(pair)[:])
            x_codes[pair] = codes
            x_scales[pair] = scales

        def multiply(pair):
            if not 0 <= pair < PAIRS:
                return
            view = place(pair)[1]
            codes = x_codes.pop(pair)
            scales = x_scales.pop(pair)
            acc = psum_m.tile([P, PAIR, 2 * F], F32, name="acc")
            for i in range(PAIR):
                for g in range(PASSES):
                    rows = slice((i * PASSES + g) * P, (i * PASSES + g + 1) * P)
                    cols = slice(g * 2 * F, (g + 1) * 2 * F)
                    nc.tensor.matmul_mx(
                        out=acc[:, i, :],
                        lhsT=codes[:, rows].bitcast(FP8X4),
                        lhsT_scale=scales[:, rows],
                        rhs=w_codes[view][:, cols].bitcast(FP8X4),
                        rhs_scale=w_scales[view][:, cols],
                        start=(g == 0),
                        stop=(g == PASSES - 1),
                    )
            products[pair] = acc

        def sum_an(pair, on_scalar):
            if not 0 <= pair < PAIRS or on_scalar != (pair % SCALAR_SHARE == 0 or pair >= PAIRS - SCALAR_TAIL):
                return
            group, view, half = place(pair)
            block, member = divmod(group, span(view))
            if (block, view) not in an_sums:
                an_sums[block, view] = work.tile([P, span(view) * CHUNK], F32, name="an_sum_%d" % span(view))
            first = member * CHUNK + half * PAIR
            if on_scalar:
                for i in range(PAIR):
                    an_copy = work.tile([P, F], BF16, name="an_copy")
                    nc.scalar.activation(
                        out=an_copy[:],
                        in_=products[pair][:, i, F : 2 * F],
                        func=mybir.ActivationFunctionType.Copy,
                        accum_out=an_sums[block, view][:, first + i : first + i + 1],
                    )
                return
            nc.vector.tensor_reduce(
                out=an_sums[block, view][:, first : first + PAIR],
                in_=products[pair][:, :, F : 2 * F],
                axis=mybir.AxisListType.X,
                op=ADD,
            )

        def sum_triples(pair):
            if not 0 <= pair < PAIRS:
                return
            group, view, half = place(pair)
            block, member = divmod(group, span(view))
            if member == 0 and half == 0:
                triples[block, view] = work.tile(
                    [P, span(view) * CHUNK, WHOLE], F32, name="triple_sums_%d" % span(view)
                )
            tile = member * CHUNK + half * PAIR
            first = FIRST_TRIPLE[view]
            nc.vector.tensor_reduce(
                out=triples[block, view][:, tile : tile + PAIR, :],
                in_=products[pair][:, :, first : first + 3 * WHOLE].rearrange("p i (j s) -> p i j s", s=VIEWS),
                axis=mybir.AxisListType.X,
                op=ADD,
            )

        def scale_edges(pair):
            if not 0 <= pair < PAIRS:
                return
            group, view, half = place(pair)
            block, member = divmod(group, span(view))
            tile = member * CHUNK + half * PAIR
            first = group * CHUNK + half * PAIR
            nc.vector.scalar_tensor_tensor(
                out=edge_sb[:, first : first + PAIR, 2 * view : 2 * view + 2],
                in0=products.pop(pair)[:, :, EDGES[view]],
                scalar=1.0 / (F * VIEWS),
                in1=an_sums[block, view][:, tile : tile + PAIR].unsqueeze(2).to_broadcast([P, PAIR, 2]),
                op0=MULT,
                op1=MULT,
            )

        def scale(pair):
            if not 0 <= pair < PAIRS:
                return
            group, view, half = place(pair)
            block, member = divmod(group, span(view))
            if half != HALVES - 1 or member != span(view) - 1:
                return
            count = span(view) * CHUNK
            tiles = slice(block * count, (block + 1) * count)
            first = (WHOLE + 1) * view
            nc.vector.scalar_tensor_tensor(
                out=out_sb[:, tiles, first : first + WHOLE],
                in0=triples.pop((block, view))[:],
                scalar=1.0 / (F * VIEWS),
                in1=an_sums.pop((block, view))[:].unsqueeze(2).to_broadcast([P, count, WHOLE]),
                op0=MULT,
                op1=MULT,
            )
            if view == VIEWS - 1:
                nc.vector.tensor_reduce(
                    out=out_sb[:, tiles, WHOLE : 2 * WHOLE + 2 : WHOLE + 1],
                    in_=edge_sb[:, tiles].rearrange("p i (j s) -> p i j s", s=VIEWS),
                    axis=mybir.AxisListType.X,
                    op=ADD,
                )
                nc.sync.dma_start(
                    out=out_rows[:, group * CHUNK * F : (group + 1) * CHUNK * F],
                    in_=out_sb[:, tiles].rearrange("p i j -> p (i j)"),
                )

        with tc.manual_schedule():
            for chunk in range(X_BUFS):
                load_x(chunk, pieces=CHUNK if chunk == 0 else HALVES, weights_after=1 if chunk == 0 else None)
            load_weights(1)
            for first in range(0, PAIRS + SCALE_LAG + 1, RUN):
                run = range(first, first + RUN)
                for pair in run:
                    sum_an(pair - SCALE_LAG, on_scalar=True)
                for pair in run:
                    transpose(pair)
                for pair in run:
                    sum_an(pair - SCALE_LAG, on_scalar=False)
                    quantise(pair - RUN)
                    if pair == RUN - 1:
                        for g in range(PASSES):
                            group_weights(0, g)
                        quantise_weights(0)
                    view, step = divmod(pair + 1, VIEW_PAIRS)
                    if 0 < view < VIEWS and step <= PASSES:
                        if step < PASSES:
                            group_weights(view, step)
                        else:
                            quantise_weights(view)
                    sum_triples(pair - SCALE_LAG)
                    scale_edges(pair - SCALE_LAG)
                    scale(pair - SCALE_LAG - 1)
                for pair in run:
                    multiply(pair - LAG)
